import numpy as np
import ml_dtypes

BF16 = ml_dtypes.bfloat16


def bf(x):
    return np.asarray(x, np.float32).astype(BF16)


def f32(x):
    return np.asarray(x, np.float32)


def f64(x):
    return np.asarray(x).astype(np.float64)


def striped(idx):
    return np.tile(idx.reshape(-1, 16).T, (8, 1))


C, S, N, K, B, BLOCK, RANK, T = 512, 1024, 256, 2, 4, 128, 128, 128


def setup_inputs():
    return {
        "base": f32(np.random.standard_normal((C, S))),
        "x": bf(np.random.standard_normal((C, N))),
        "shared": f32(np.random.standard_normal((C, N))),
        "rule_down": bf(np.random.standard_normal((K, BLOCK, RANK)) / np.sqrt(BLOCK)),
        "rule_up": bf(np.random.standard_normal((K, RANK, BLOCK)) / np.sqrt(RANK)),
        "logits": f32(np.random.standard_normal((K, B)) / np.sqrt(B)),
        "offs": striped(np.random.permutation(S)[:N]),
    }


def reference(base, x, shared, rule_down, rule_up, logits, offs):
    idx = offs[:16].T.reshape(-1)
    xb = f64(x).reshape(B, BLOCK, K, T)
    hidden = np.einsum('bikt,kir->kbrt', xb, f64(rule_down))
    adapter = np.einsum('kbrt,kru->bukt', hidden, f64(rule_up))
    e = np.exp(f64(logits) * np.sqrt(B))
    sel = e / e.sum(axis=1, keepdims=True)
    weighted = (adapter * sel.T[:, None, :, None]).reshape(C, N)
    out = f64(base).copy()
    out[:, idx] = f64(shared) + weighted
    return out

@@ -1,0 +1,77 @@
+import concourse.mybir as mybir
+
+BF16, F32, U16 = mybir.dt.bfloat16, mybir.dt.float32, mybir.dt.uint16
+ADD, SUBTRACT, MULT = mybir.AluOpType.add, mybir.AluOpType.subtract, mybir.AluOpType.mult
+COPY, EXP = mybir.ActivationFunctionType.Copy, mybir.ActivationFunctionType.Exp
+X_AXIS = mybir.AxisListType.X
+
+P = 128
+B = 4
+K = 2
+T = 128
+N = K * T
+S = 1024
+
+FLOPS = 2 * 2 * (B * P) * N * P
+
+
+def tile_ruleawareprojection_s_kernel(tc, base, x, shared, rule_down, rule_up, logits, offs, out):
+    nc = tc.nc
+    with (
+        tc.tile_pool(name="held", bufs=1) as held,
+        tc.tile_pool(name="blocks", bufs=B) as blocks,
+        tc.psum_pool(name="psum", bufs=2) as psum,
+    ):
+        down = held.tile([P, K, P], BF16, name="down")
+        nc.scalar.dma_start(down[:], rule_down.rearrange("k i r -> i k r"))
+        up = held.tile([P, K, P], BF16, name="up")
+        nc.scalar.dma_start(up[:], rule_up.rearrange("k r u -> r k u"))
+        logit = held.tile([P, K * B], F32, name="logit")
+        nc.scalar.dma_start(logit[:], logits.rearrange("k b -> (k b)").partition_broadcast(P))
+        offsets = held.tile([P, N // 16], U16, name="offsets")
+        nc.sync.dma_start(offsets[:], offs)
+
+        x_blocks, shared_blocks, windows = [], [], []
+        for b in range(B):
+            rows = slice(b * P, (b + 1) * P)
+            x_b = blocks.tile([P, N], BF16, name="x_b")
+            nc.sync.dma_start(x_b[:], x[rows, :])
+            window = blocks.tile([P, S], F32, name="window")
+            nc.sync.dma_start(window[:], base[rows, :])
+            shared_b = blocks.tile([P, N], F32, name="shared_b")
+            nc.scalar.dma_start(shared_b[:], shared[rows, :])
+            x_blocks.append(x_b)
+            shared_blocks.append(shared_b)
+            windows.append(window)
+
+        logit_kb = logit[:].rearrange("p (k b) -> p k b", k=K)
+        top = held.tile([P, K], F32, name="top")
+        nc.vector.reduce_max(top[:], logit_kb, axis=X_AXIS)
+        shifted = held.tile([P, K, B], F32, name="shifted")
+        nc.vector.tensor_tensor(shifted[:], logit_kb, top[:].unsqueeze(2).to_broadcast([P, K, B]), SUBTRACT)
+        grown = held.tile([P, K, B], F32, name="grown")
+        nc.scalar.activation(grown[:], shifted[:], EXP, scale=2.0)
+        total = held.tile([P, K], F32, name="total")
+        nc.vector.reduce_sum(total[:], grown[:], axis=X_AXIS)
+        inverse = held.tile([P, K], F32, name="inverse")
+        nc.vector.reciprocal(inverse[:], total[:])
+        sel = held.tile([P, K, B], F32, name="sel")
+        nc.vector.tensor_tensor(sel[:], grown[:], inverse[:].unsqueeze(2).to_broadcast([P, K, B]), MULT)
+
+        for b in range(B):
+            hidden_sum = psum.tile([P, N], F32, name="hidden_sum")
+            for k in range(K):
+                tokens = slice(k * T, (k + 1) * T)
+                nc.tensor.matmul(hidden_sum[:, tokens], down[:, k, :], x_blocks[b][:, tokens], start=True, stop=True)
+            hidden = blocks.tile([P, N], BF16, name="hidden")
+            nc.scalar.activation(hidden[:], hidden_sum[:], COPY)
+
+            adapter = psum.tile([P, N], F32, name="adapter")
+            weighted = blocks.tile([P, N], F32, name="weighted")
+            for k in range(K):
+                tokens = slice(k * T, (k + 1) * T)
+                nc.tensor.matmul(adapter[:, tokens], up[:, k, :], hidden[:, tokens], start=True, stop=True)
+                nc.scalar.activation(weighted[:, tokens], adapter[:, tokens], COPY, scale=sel[:, k, b : b + 1])
+
+            nc.vector.tensor_tensor(windows[b][:].indirect(offsets[:]), shared_blocks[b][:], weighted[:], ADD)
+            nc.sync.dma_start(out[b * P : (b + 1) * P, :], windows[b][:])

@@ -22,25 +22,23 @@ def tile_ruleawareprojection_s_kernel(tc, base, x, shared, rule_down, rule_up, l
         tc.tile_pool(name="blocks", bufs=B) as blocks,
         tc.psum_pool(name="psum", bufs=2) as psum,
     ):
-        down = held.tile([P, K, P], BF16, name="down")
-        nc.scalar.dma_start(down[:], rule_down.rearrange("k i r -> i k r"))
-        up = held.tile([P, K, P], BF16, name="up")
-        nc.scalar.dma_start(up[:], rule_up.rearrange("k r u -> r k u"))
         logit = held.tile([P, K * B], F32, name="logit")
         nc.scalar.dma_start(logit[:], logits.rearrange("k b -> (k b)").partition_broadcast(P))
+        down = held.tile([P, K, P], BF16, name="down")
+        nc.sync.dma_start(down[:], rule_down.rearrange("k i r -> i k r"))
+        x_all = held.tile([P, B, N], BF16, name="x_all")
+        nc.sync.dma_start(x_all[:], x.rearrange("(b i) j -> i b j", i=P))
+        up = held.tile([P, K, P], BF16, name="up")
+        nc.scalar.dma_start(up[:], rule_up.rearrange("k r u -> r k u"))
         offsets = held.tile([P, N // 16], U16, name="offsets")
         nc.sync.dma_start(offsets[:], offs)
-
-        x_blocks, shared_blocks, windows = [], [], []
+        shared_blocks, windows = [], []
         for b in range(B):
             rows = slice(b * P, (b + 1) * P)
-            x_b = blocks.tile([P, N], BF16, name="x_b")
-            nc.sync.dma_start(x_b[:], x[rows, :])
+            shared_b = blocks.tile([P, N], F32, name="shared_b")
+            nc.sync.dma_start(shared_b[:], shared[rows, :])
             window = blocks.tile([P, S], F32, name="window")
             nc.sync.dma_start(window[:], base[rows, :])
-            shared_b = blocks.tile([P, N], F32, name="shared_b")
-            nc.scalar.dma_start(shared_b[:], shared[rows, :])
-            x_blocks.append(x_b)
             shared_blocks.append(shared_b)
             windows.append(window)
 
@@ -62,7 +60,7 @@ def tile_ruleawareprojection_s_kernel(tc, base, x, shared, rule_down, rule_up, l
             hidden_sum = psum.tile([P, N], F32, name="hidden_sum")
             for k in range(K):
                 tokens = slice(k * T, (k + 1) * T)
-                nc.tensor.matmul(hidden_sum[:, tokens], down[:, k, :], x_blocks[b][:, tokens], start=True, stop=True)
+                nc.tensor.matmul(hidden_sum[:, tokens], down[:, k, :], x_all[:, b, tokens], start=True, stop=True)
             hidden = blocks.tile([P, N], BF16, name="hidden")
             nc.scalar.activation(hidden[:], hidden_sum[:], COPY)
 

@@ -27,9 +27,10 @@ def tile_ruleawareprojection_s_kernel(tc, base, x, shared, rule_down, rule_up, l
         down = held.tile([P, K, P], BF16, name="down")
         nc.sync.dma_start(down[:], rule_down.rearrange("k i r -> i k r"))
         x_all = held.tile([P, B, N], BF16, name="x_all")
-        nc.sync.dma_start(x_all[:], x.rearrange("(b i) j -> i b j", i=P))
+        nc.sync.dma_start(x_all[:, 0, :], x[0:P, :])
         up = held.tile([P, K, P], BF16, name="up")
         nc.scalar.dma_start(up[:], rule_up.rearrange("k r u -> r k u"))
+        nc.sync.dma_start(x_all[:, 1:B, :], x[P : B * P, :].rearrange("(b i) j -> i b j", i=P))
         offsets = held.tile([P, N // 16], U16, name="offsets")
         nc.sync.dma_start(offsets[:], offs)
         shared_blocks, windows = [], []
@@ -57,19 +58,19 @@ def tile_ruleawareprojection_s_kernel(tc, base, x, shared, rule_down, rule_up, l
         nc.vector.tensor_tensor(sel[:], grown[:], inverse[:].unsqueeze(2).to_broadcast([P, K, B]), MULT)
 
         for b in range(B):
-            hidden_sum = psum.tile([P, N], F32, name="hidden_sum")
+            hidden_sums = [psum.tile([P, T], F32, name=f"hidden_sum{k}") for k in range(K)]
             for k in range(K):
-                tokens = slice(k * T, (k + 1) * T)
-                nc.tensor.matmul(hidden_sum[:, tokens], down[:, k, :], x_all[:, b, tokens], start=True, stop=True)
-            hidden = blocks.tile([P, N], BF16, name="hidden")
-            nc.scalar.activation(hidden[:], hidden_sum[:], COPY)
+                nc.tensor.matmul(hidden_sums[k][:], down[:, k, :], x_all[:, b, k * T : (k + 1) * T], start=True, stop=True)
+            hidden = blocks.tile([P, K, T], BF16, name="hidden")
+            for k in range(K):
+                nc.scalar.activation(hidden[:, k, :], hidden_sums[k][:], COPY)
 
-            adapter = psum.tile([P, N], F32, name="adapter")
+            adapters = [psum.tile([P, T], F32, name=f"adapter{k}") for k in range(K)]
+            for k in range(K):
+                nc.tensor.matmul(adapters[k][:], up[:, k, :], hidden[:, k, :], start=True, stop=True)
             weighted = blocks.tile([P, N], F32, name="weighted")
             for k in range(K):
-                tokens = slice(k * T, (k + 1) * T)
-                nc.tensor.matmul(adapter[:, tokens], up[:, k, :], hidden[:, tokens], start=True, stop=True)
-                nc.scalar.activation(weighted[:, tokens], adapter[:, tokens], COPY, scale=sel[:, k, b : b + 1])
+                nc.scalar.activation(weighted[:, k * T : (k + 1) * T], adapters[k][:], COPY, scale=sel[:, k, b : b + 1])
 
             nc.vector.tensor_tensor(windows[b][:].indirect(offsets[:]), shared_blocks[b][:], weighted[:], ADD)
             nc.sync.dma_start(out[b * P : (b + 1) * P, :], windows[b][:])

@@ -23,14 +23,13 @@ def tile_ruleawareprojection_s_kernel(tc, base, x, shared, rule_down, rule_up, l
         tc.psum_pool(name="psum", bufs=2) as psum,
     ):
         logit = held.tile([P, K * B], F32, name="logit")
-        nc.scalar.dma_start(logit[:], logits.rearrange("k b -> (k b)").partition_broadcast(P))
+        nc.sync.dma_start(logit[:], logits.rearrange("k b -> (k b)").partition_broadcast(P))
         down = held.tile([P, K, P], BF16, name="down")
         nc.sync.dma_start(down[:], rule_down.rearrange("k i r -> i k r"))
         x_all = held.tile([P, B, N], BF16, name="x_all")
         nc.sync.dma_start(x_all[:, 0, :], x[0:P, :])
         up = held.tile([P, K, P], BF16, name="up")
-        nc.scalar.dma_start(up[:], rule_up.rearrange("k r u -> r k u"))
-        nc.sync.dma_start(x_all[:, 1:B, :], x[P : B * P, :].rearrange("(b i) j -> i b j", i=P))
+        nc.sync.dma_start(up[:], rule_up.rearrange("k r u -> r k u"))
         offsets = held.tile([P, N // 16], U16, name="offsets")
         nc.sync.dma_start(offsets[:], offs)
         shared_blocks, windows = [], []
@@ -40,6 +39,8 @@ def tile_ruleawareprojection_s_kernel(tc, base, x, shared, rule_down, rule_up, l
             nc.sync.dma_start(shared_b[:], shared[rows, :])
             window = blocks.tile([P, S], F32, name="window")
             nc.sync.dma_start(window[:], base[rows, :])
+            if b == 0:
+                nc.sync.dma_start(x_all[:, 1:B, :], x[P : B * P, :].rearrange("(b i) j -> i b j", i=P))
             shared_blocks.append(shared_b)
             windows.append(window)
 

@@ -26,21 +26,21 @@ def tile_ruleawareprojection_s_kernel(tc, base, x, shared, rule_down, rule_up, l
         nc.sync.dma_start(logit[:], logits.rearrange("k b -> (k b)").partition_broadcast(P))
         down = held.tile([P, K, P], BF16, name="down")
         nc.sync.dma_start(down[:], rule_down.rearrange("k i r -> i k r"))
-        x_all = held.tile([P, B, N], BF16, name="x_all")
-        nc.sync.dma_start(x_all[:, 0, :], x[0:P, :])
-        up = held.tile([P, K, P], BF16, name="up")
-        nc.sync.dma_start(up[:], rule_up.rearrange("k r u -> r k u"))
-        offsets = held.tile([P, N // 16], U16, name="offsets")
-        nc.sync.dma_start(offsets[:], offs)
-        shared_blocks, windows = [], []
+        x_blocks, shared_blocks, windows = [], [], []
         for b in range(B):
             rows = slice(b * P, (b + 1) * P)
+            x_b = blocks.tile([P, N], BF16, name="x_b")
+            nc.sync.dma_start(x_b[:], x[rows, :])
+            if b == 0:
+                up = held.tile([P, K, P], BF16, name="up")
+                nc.sync.dma_start(up[:], rule_up.rearrange("k r u -> r k u"))
+                offsets = held.tile([P, N // 16], U16, name="offsets")
+                nc.sync.dma_start(offsets[:], offs)
             shared_b = blocks.tile([P, N], F32, name="shared_b")
             nc.sync.dma_start(shared_b[:], shared[rows, :])
             window = blocks.tile([P, S], F32, name="window")
             nc.sync.dma_start(window[:], base[rows, :])
-            if b == 0:
-                nc.sync.dma_start(x_all[:, 1:B, :], x[P : B * P, :].rearrange("(b i) j -> i b j", i=P))
+            x_blocks.append(x_b)
             shared_blocks.append(shared_b)
             windows.append(window)
 
@@ -61,7 +61,7 @@ def tile_ruleawareprojection_s_kernel(tc, base, x, shared, rule_down, rule_up, l
         for b in range(B):
             hidden_sums = [psum.tile([P, T], F32, name=f"hidden_sum{k}") for k in range(K)]
             for k in range(K):
-                nc.tensor.matmul(hidden_sums[k][:], down[:, k, :], x_all[:, b, k * T : (k + 1) * T], start=True, stop=True)
+                nc.tensor.matmul(hidden_sums[k][:], down[:, k, :], x_blocks[b][:, k * T : (k + 1) * T], start=True, stop=True)
             hidden = blocks.tile([P, K, T], BF16, name="hidden")
             for k in range(K):
                 nc.scalar.activation(hidden[:, k, :], hidden_sums[k][:], COPY)

@@ -11,6 +11,7 @@ K = 2
 T = 128
 N = K * T
 S = 1024
+ROW_ALIGN = 4 * S
 
 FLOPS = 2 * 2 * (B * P) * N * P
 
@@ -29,16 +30,16 @@ def tile_ruleawareprojection_s_kernel(tc, base, x, shared, rule_down, rule_up, l
         x_blocks, shared_blocks, windows = [], [], []
         for b in range(B):
             rows = slice(b * P, (b + 1) * P)
-            x_b = blocks.tile([P, N], BF16, name="x_b")
+            x_b = blocks.tile([P, N], BF16, name="x_b", align_bytes=ROW_ALIGN)
             nc.sync.dma_start(x_b[:], x[rows, :])
             if b == 0:
                 up = held.tile([P, K, P], BF16, name="up")
                 nc.sync.dma_start(up[:], rule_up.rearrange("k r u -> r k u"))
                 offsets = held.tile([P, N // 16], U16, name="offsets")
                 nc.sync.dma_start(offsets[:], offs)
-            shared_b = blocks.tile([P, N], F32, name="shared_b")
+            shared_b = blocks.tile([P, N], F32, name="shared_b", align_bytes=ROW_ALIGN)
             nc.sync.dma_start(shared_b[:], shared[rows, :])
-            window = blocks.tile([P, S], F32, name="window")
+            window = blocks.tile([P, S], F32, name="window", align_bytes=ROW_ALIGN)
             nc.sync.dma_start(window[:], base[rows, :])
             x_blocks.append(x_b)
             shared_blocks.append(shared_b)

@@ -25,7 +25,7 @@ def tile_ruleawareprojection_s_kernel(tc, base, x, shared, rule_down, rule_up, l
     ):
         logit = held.tile([P, K * B], F32, name="logit")
         nc.sync.dma_start(logit[:], logits.rearrange("k b -> (k b)").partition_broadcast(P))
-        down = held.tile([P, K, P], BF16, name="down")
+        down = held.tile([P, K, P], BF16, name="down", align_bytes=ROW_ALIGN)
         nc.sync.dma_start(down[:], rule_down.rearrange("k i r -> i k r"))
         x_blocks, shared_blocks, windows = [], [], []
         for b in range(B):
@@ -33,7 +33,7 @@ def tile_ruleawareprojection_s_kernel(tc, base, x, shared, rule_down, rule_up, l
             x_b = blocks.tile([P, N], BF16, name="x_b", align_bytes=ROW_ALIGN)
             nc.sync.dma_start(x_b[:], x[rows, :])
             if b == 0:
-                up = held.tile([P, K, P], BF16, name="up")
+                up = held.tile([P, K, P], BF16, name="up", align_bytes=ROW_ALIGN)
                 nc.sync.dma_start(up[:], rule_up.rearrange("k r u -> r k u"))
                 offsets = held.tile([P, N // 16], U16, name="offsets")
                 nc.sync.dma_start(offsets[:], offs)

@@ -11,7 +11,7 @@ K = 2
 T = 128
 N = K * T
 S = 1024
-ROW_ALIGN = 4 * S
+ROW_ALIGN = 256
 
 FLOPS = 2 * 2 * (B * P) * N * P
 

@@ -57,7 +57,6 @@ def tile_ruleawareprojection_s_kernel(tc, base, x, shared, rule_down, rule_up, l
         inverse = held.tile([P, K], F32, name="inverse")
         nc.vector.reciprocal(inverse[:], total[:])
         sel = held.tile([P, K, B], F32, name="sel")
-        nc.vector.tensor_tensor(sel[:], grown[:], inverse[:].unsqueeze(2).to_broadcast([P, K, B]), MULT)
 
         for b in range(B):
             hidden_sums = [psum.tile([P, T], F32, name=f"hidden_sum{k}") for k in range(K)]
@@ -71,8 +70,16 @@ def tile_ruleawareprojection_s_kernel(tc, base, x, shared, rule_down, rule_up, l
             for k in range(K):
                 nc.tensor.matmul(adapters[k][:], up[:, k, :], hidden[:, k, :], start=True, stop=True)
             weighted = blocks.tile([P, N], F32, name="weighted")
-            for k in range(K):
-                nc.scalar.activation(weighted[:, k * T : (k + 1) * T], adapters[k][:], COPY, scale=sel[:, k, b : b + 1])
+            if b == 0:
+                for k in range(K):
+                    nc.vector.tensor_scalar(
+                        weighted[:, k * T : (k + 1) * T], adapters[k][:], grown[:, k, 0:1], inverse[:, k : k + 1], MULT, MULT
+                    )
+                for k in range(K):
+                    nc.scalar.activation(sel[:, k, :], grown[:, k, :], COPY, scale=inverse[:, k : k + 1])
+            else:
+                for k in range(K):
+                    nc.scalar.activation(weighted[:, k * T : (k + 1) * T], adapters[k][:], COPY, scale=sel[:, k, b : b + 1])
 
             nc.vector.tensor_tensor(windows[b][:].indirect(offsets[:]), shared_blocks[b][:], weighted[:], ADD)
             nc.sync.dma_start(out[b * P : (b + 1) * P, :], windows[b][:])

@@ -27,21 +27,21 @@ def tile_ruleawareprojection_s_kernel(tc, base, x, shared, rule_down, rule_up, l
         nc.sync.dma_start(logit[:], logits.rearrange("k b -> (k b)").partition_broadcast(P))
         down = held.tile([P, K, P], BF16, name="down", align_bytes=ROW_ALIGN)
         nc.sync.dma_start(down[:], rule_down.rearrange("k i r -> i k r"))
-        x_blocks, shared_blocks, windows = [], [], []
+        x_blocks = [blocks.tile([P, N], BF16, name="x_b", align_bytes=ROW_ALIGN) for b in range(B)]
+        nc.sync.dma_start(x_blocks[0][:], x[0:P, :])
+        up = held.tile([P, K, P], BF16, name="up", align_bytes=ROW_ALIGN)
+        nc.sync.dma_start(up[:], rule_up.rearrange("k r u -> r k u"))
+        offsets = held.tile([P, N // 16], U16, name="offsets")
+        nc.sync.dma_start(offsets[:], offs)
+        shared_blocks, windows = [], []
         for b in range(B):
             rows = slice(b * P, (b + 1) * P)
-            x_b = blocks.tile([P, N], BF16, name="x_b", align_bytes=ROW_ALIGN)
-            nc.sync.dma_start(x_b[:], x[rows, :])
-            if b == 0:
-                up = held.tile([P, K, P], BF16, name="up", align_bytes=ROW_ALIGN)
-                nc.sync.dma_start(up[:], rule_up.rearrange("k r u -> r k u"))
-                offsets = held.tile([P, N // 16], U16, name="offsets")
-                nc.sync.dma_start(offsets[:], offs)
+            if b + 1 < B:
+                nc.sync.dma_start(x_blocks[b + 1][:], x[(b + 1) * P : (b + 2) * P, :])
             shared_b = blocks.tile([P, N], F32, name="shared_b", align_bytes=ROW_ALIGN)
             nc.sync.dma_start(shared_b[:], shared[rows, :])
             window = blocks.tile([P, S], F32, name="window", align_bytes=ROW_ALIGN)
             nc.sync.dma_start(window[:], base[rows, :])
-            x_blocks.append(x_b)
             shared_blocks.append(shared_b)
             windows.append(window)
 

@@ -1,7 +1,7 @@
 import concourse.mybir as mybir
 
 BF16, F32, U16 = mybir.dt.bfloat16, mybir.dt.float32, mybir.dt.uint16
-ADD, SUBTRACT, MULT = mybir.AluOpType.add, mybir.AluOpType.subtract, mybir.AluOpType.mult
+ADD, SUBTRACT = mybir.AluOpType.add, mybir.AluOpType.subtract
 COPY, EXP = mybir.ActivationFunctionType.Copy, mybir.ActivationFunctionType.Exp
 X_AXIS = mybir.AxisListType.X
 
@@ -46,17 +46,19 @@ def tile_ruleawareprojection_s_kernel(tc, base, x, shared, rule_down, rule_up, l
             windows.append(window)
 
         logit_kb = logit[:].rearrange("p (k b) -> p k b", k=K)
-        top = held.tile([P, K], F32, name="top")
-        nc.vector.reduce_max(top[:], logit_kb, axis=X_AXIS)
-        shifted = held.tile([P, K, B], F32, name="shifted")
-        nc.vector.tensor_tensor(shifted[:], logit_kb, top[:].unsqueeze(2).to_broadcast([P, K, B]), SUBTRACT)
-        grown = held.tile([P, K, B], F32, name="grown")
-        nc.scalar.activation(grown[:], shifted[:], EXP, scale=2.0)
-        total = held.tile([P, K], F32, name="total")
+        ahead = held.tile([P, K, B, B], F32, name="ahead")
+        nc.vector.tensor_tensor(
+            ahead[:],
+            logit_kb.unsqueeze(2).to_broadcast([P, K, B, B]),
+            logit_kb.unsqueeze(3).to_broadcast([P, K, B, B]),
+            SUBTRACT,
+        )
+        grown = held.tile([P, K, B, B], F32, name="grown")
+        nc.scalar.activation(grown[:], ahead[:], EXP, scale=2.0)
+        total = held.tile([P, K, B], F32, name="total")
         nc.vector.reduce_sum(total[:], grown[:], axis=X_AXIS)
-        inverse = held.tile([P, K], F32, name="inverse")
-        nc.vector.reciprocal(inverse[:], total[:])
         sel = held.tile([P, K, B], F32, name="sel")
+        nc.vector.reciprocal(sel[:], total[:])
 
         for b in range(B):
             hidden_sums = [psum.tile([P, T], F32, name=f"hidden_sum{k}") for k in range(K)]
@@ -70,16 +72,12 @@ def tile_ruleawareprojection_s_kernel(tc, base, x, shared, rule_down, rule_up, l
             for k in range(K):
                 nc.tensor.matmul(adapters[k][:], up[:, k, :], hidden[:, k, :], start=True, stop=True)
             weighted = blocks.tile([P, N], F32, name="weighted")
-            if b == 0:
-                for k in range(K):
-                    nc.vector.tensor_scalar(
-                        weighted[:, k * T : (k + 1) * T], adapters[k][:], grown[:, k, 0:1], inverse[:, k : k + 1], MULT, MULT
-                    )
-                for k in range(K):
-                    nc.scalar.activation(sel[:, k, :], grown[:, k, :], COPY, scale=inverse[:, k : k + 1])
-            else:
-                for k in range(K):
-                    nc.scalar.activation(weighted[:, k * T : (k + 1) * T], adapters[k][:], COPY, scale=sel[:, k, b : b + 1])
+            for k in range(K):
+                half = weighted[:, k * T : (k + 1) * T]
+                if b == 0:
+                    nc.vector.tensor_scalar_mul(half, adapters[k][:], sel[:, k, b : b + 1])
+                else:
+                    nc.scalar.activation(half, adapters[k][:], COPY, scale=sel[:, k, b : b + 1])
 
             nc.vector.tensor_tensor(windows[b][:].indirect(offsets[:]), shared_blocks[b][:], weighted[:], ADD)
             nc.sync.dma_start(out[b * P : (b + 1) * P, :], windows[b][:])

import concourse.mybir as mybir

BF16, F32, U16 = mybir.dt.bfloat16, mybir.dt.float32, mybir.dt.uint16
ADD, SUBTRACT = mybir.AluOpType.add, mybir.AluOpType.subtract
COPY, EXP = mybir.ActivationFunctionType.Copy, mybir.ActivationFunctionType.Exp
X_AXIS = mybir.AxisListType.X

P = 128
B = 4
K = 2
T = 128
N = K * T
S = 1024
ROW_ALIGN = 256

FLOPS = 2 * 2 * (B * P) * N * P


def tile_ruleawareprojection_s_kernel(tc, base, x, shared, rule_down, rule_up, logits, offs, out):
    nc = tc.nc
    with (
        tc.tile_pool(name="held", bufs=1) as held,
        tc.tile_pool(name="blocks", bufs=B) as blocks,
        tc.psum_pool(name="psum", bufs=2) as psum,
    ):
        logit = held.tile([P, K * B], F32, name="logit")
        nc.sync.dma_start(logit[:], logits.rearrange("k b -> (k b)").partition_broadcast(P))
        down = held.tile([P, K, P], BF16, name="down", align_bytes=ROW_ALIGN)
        nc.sync.dma_start(down[:], rule_down.rearrange("k i r -> i k r"))
        x_blocks = [blocks.tile([P, N], BF16, name="x_b", align_bytes=ROW_ALIGN) for b in range(B)]
        nc.sync.dma_start(x_blocks[0][:], x[0:P, :])
        up = held.tile([P, K, P], BF16, name="up", align_bytes=ROW_ALIGN)
        nc.sync.dma_start(up[:], rule_up.rearrange("k r u -> r k u"))
        offsets = held.tile([P, N // 16], U16, name="offsets")
        nc.sync.dma_start(offsets[:], offs)
        shared_blocks, windows = [], []
        for b in range(B):
            rows = slice(b * P, (b + 1) * P)
            if b + 1 < B:
                nc.sync.dma_start(x_blocks[b + 1][:], x[(b + 1) * P : (b + 2) * P, :])
            shared_b = blocks.tile([P, N], F32, name="shared_b", align_bytes=ROW_ALIGN)
            nc.sync.dma_start(shared_b[:], shared[rows, :])
            window = blocks.tile([P, S], F32, name="window", align_bytes=ROW_ALIGN)
            nc.sync.dma_start(window[:], base[rows, :])
            shared_blocks.append(shared_b)
            windows.append(window)

        logit_kb = logit[:].rearrange("p (k b) -> p k b", k=K)
        ahead = held.tile([P, K, B, B], F32, name="ahead")
        nc.vector.tensor_tensor(
            ahead[:],
            logit_kb.unsqueeze(2).to_broadcast([P, K, B, B]),
            logit_kb.unsqueeze(3).to_broadcast([P, K, B, B]),
            SUBTRACT,
        )
        grown = held.tile([P, K, B, B], F32, name="grown")
        nc.scalar.activation(grown[:], ahead[:], EXP, scale=2.0)
        total = held.tile([P, K, B], F32, name="total")
        nc.vector.reduce_sum(total[:], grown[:], axis=X_AXIS)
        sel = held.tile([P, K, B], F32, name="sel")
        nc.vector.reciprocal(sel[:], total[:])

        for b in range(B):
            hidden_sums = [psum.tile([P, T], F32, name=f"hidden_sum{k}") for k in range(K)]
            for k in range(K):
                nc.tensor.matmul(hidden_sums[k][:], down[:, k, :], x_blocks[b][:, k * T : (k + 1) * T], start=True, stop=True)
            hidden = blocks.tile([P, K, T], BF16, name="hidden")
            for k in range(K):
                nc.scalar.activation(hidden[:, k, :], hidden_sums[k][:], COPY)

            adapters = [psum.tile([P, T], F32, name=f"adapter{k}") for k in range(K)]
            for k in range(K):
                nc.tensor.matmul(adapters[k][:], up[:, k, :], hidden[:, k, :], start=True, stop=True)
            weighted = blocks.tile([P, N], F32, name="weighted")
            for k in range(K):
                half = weighted[:, k * T : (k + 1) * T]
                if b == 0:
                    nc.vector.tensor_scalar_mul(half, adapters[k][:], sel[:, k, b : b + 1])
                else:
                    nc.scalar.activation(half, adapters[k][:], COPY, scale=sel[:, k, b : b + 1])

            nc.vector.tensor_tensor(windows[b][:].indirect(offsets[:]), shared_blocks[b][:], weighted[:], ADD)
            nc.sync.dma_start(out[b * P : (b + 1) * P, :], windows[b][:])
